import numpy as np
import ml_dtypes


def mxq(x, axis, fmt="e4m3"):
    dtype, down = {"e4m3": (ml_dtypes.float8_e4m3fn, 7), "e5m2": (ml_dtypes.float8_e5m2, 14)}[fmt]
    v = np.moveaxis(np.asarray(x, np.float32).astype(ml_dtypes.bfloat16).astype(np.float64), axis, -1)
    blocks = v.reshape(v.shape[:-1] + (-1, 32))
    amax = np.abs(blocks).max(-1, keepdims=True)
    byte = np.maximum(np.where(amax > 0, np.frexp(amax)[1] - 1 + 127, 0) - down, 1)
    scale = np.exp2(byte - 127.0)
    codes = (blocks / scale).astype(np.float32).astype(dtype).astype(np.float64)
    return np.moveaxis((codes * scale).reshape(v.shape), -1, axis)


WIDE = False


def mx_kscale(k):
    if not WIDE:
        return np.ones(k)
    levels = np.array([10, -10, 5, -5, 0])
    if k % 512:
        return np.exp2(np.random.permutation(np.resize(levels, k // 32))).repeat(32)
    a = np.empty((k // 512, 16))
    for p in range(k // 512):
        a[p, :8] = np.random.permutation(np.resize(levels, 8))
        for g in range(8):
            far = levels[np.abs(levels - a[p, g]) >= 10]
            a[p, g + 8] = far[np.random.randint(len(far))]
    return np.exp2(a.ravel()).repeat(32)


BF16 = ml_dtypes.bfloat16


def bf(x):
    return np.asarray(x, np.float32).astype(BF16)


def f64(x):
    return np.asarray(x).astype(np.float64)


B, IN, H = 128, 512, 512


def sigmoid(v):
    return 1.0 / (1.0 + np.exp(-v))


def setup_inputs():
    s, t = mx_kscale(IN), mx_kscale(H)
    a = np.sqrt(2.0 / (IN + H))
    d = 0.3 + np.random.standard_normal((B, H)) * 1.6
    return {
        "x": bf(np.random.standard_normal((B, IN)) * s),
        "h_prev": bf(np.random.standard_normal((B, H)) * t),
        "c_prev": bf(np.random.standard_normal((B, H))),
        "n_prev": bf(1.0 + np.random.standard_normal((B, H)) * 0.1),
        "i_prime": bf(np.exp(np.minimum(d, 0.0))),
        "f_prime": bf(np.exp(np.minimum(-d, 0.0))),
        "Wz_x": bf(np.random.standard_normal((H, IN)) * a / s),
        "b_z": bf(np.random.standard_normal(H) * 0.3),
        "Wz_h": bf(np.random.standard_normal((H, H)) * a / t),
        "Wo_x": bf(np.random.standard_normal((H, IN)) * a / s),
        "b_o": bf(np.random.standard_normal(H) * 0.3),
        "Wo_h": bf(np.random.standard_normal((H, H)) * a / t),
    }


def reference(x, h_prev, c_prev, n_prev, i_prime, f_prime, Wz_x, b_z, Wz_h, Wo_x, b_o, Wo_h):
    xq = mxq(f64(x), 1, "e4m3")
    hq = mxq(f64(h_prev), 1, "e4m3")
    z_aff = (xq @ mxq(f64(Wz_x), 1, "e4m3").T) + f64(b_z) + (hq @ mxq(f64(Wz_h), 1, "e4m3").T)
    o_aff = (xq @ mxq(f64(Wo_x), 1, "e4m3").T) + f64(b_o) + (hq @ mxq(f64(Wo_h), 1, "e4m3").T)
    z = np.tanh(z_aff)
    c_t = f64(f_prime) * f64(c_prev) + f64(i_prime) * z
    n_t = f64(f_prime) * f64(n_prev) + f64(i_prime)
    h_t = sigmoid(o_aff) * (c_t / np.maximum(n_t, 1e-6))
    return h_t, c_t

@@ -1,0 +1,233 @@
+from contextlib import ExitStack
+
+import concourse.mybir as mybir
+from concourse.masks import make_identity
+
+F32 = mybir.dt.float32
+BF16 = mybir.dt.bfloat16
+U32 = mybir.dt.uint32
+U8 = mybir.dt.uint8
+FP8X4 = mybir.dt.float8_e4m3fn_x4
+ALU = mybir.AluOpType
+ACT = mybir.ActivationFunctionType
+
+P = 128
+K = 512
+H = 512
+WORDS = K // 2
+HALF_GATE = 2 * P
+QUARTERS = 4
+PSUM_BANKS = 8
+SUM_BANKS = 2
+
+FLOPS = 2 * P * (2 * K) * (2 * H)
+
+
+def turn_two_panels(nc, turned_pool, grouped_pool, ident, words, first_panel):
+    bank = turned_pool.tile([P, 2 * WORDS], F32)
+    for piece in range(4):
+        first_word = (first_panel + piece // 2) * WORDS + piece % 2
+        nc.tensor.transpose(
+            bank[:, piece * P : (piece + 1) * P],
+            words[:, first_word : first_word + WORDS - 1 : 2],
+            ident[:],
+        )
+    grouped = grouped_pool.tile([P, 4 * HALF_GATE], BF16, align_bytes=64)
+    nc.scalar.copy(
+        out=grouped[:].bitcast(F32).rearrange("q (a c u) -> q a c u", a=2, u=2),
+        in_=bank[:].rearrange("q (a u c) -> q a c u", a=2, u=2),
+    )
+    return grouped
+
+
+def tile_slstmlayer_pb_s_kernel(
+    tc, x, h_prev, c_prev, n_prev, i_prime, f_prime, Wz_x, b_z, Wz_h, Wo_x, b_o, Wo_h, out_0, out_1
+):
+    nc = tc.nc
+    half_gates = (("z", 0), ("z", 1), ("o", 0), ("o", 1))
+    weights = {("z", "x"): Wz_x, ("z", "h"): Wz_h, ("o", "x"): Wo_x, ("o", "h"): Wo_h}
+    sides = ("x", "h")
+
+    with ExitStack() as ctx:
+        keep = ctx.enter_context(tc.tile_pool(name="keep", bufs=1))
+        stage = ctx.enter_context(tc.tile_pool(name="stage", bufs=6))
+        turned_pool = ctx.enter_context(tc.psum_pool(name="turned", bufs=PSUM_BANKS - SUM_BANKS))
+        sums = ctx.enter_context(tc.psum_pool(name="sums", bufs=SUM_BANKS))
+        ctx.enter_context(tc.manual_schedule())
+
+        bias_rows = keep.tile([P, 2 * P], BF16)
+        nc.gpsimd.memset(bias_rows[:].bitcast(F32), 0.0)
+        ident = keep.tile([P, P], F32)
+        make_identity(nc, ident[:])
+
+        nc.sync.dma_start(out=bias_rows[0:2, :], in_=b_z.rearrange("(r c) -> r c", r=2))
+        nc.sync.dma_start(out=bias_rows[2:4, :], in_=b_o.rearrange("(r c) -> r c", r=2))
+
+        def load_rows(name, source):
+            rows = keep.tile([P, H], BF16, name=name)
+            nc.sync.dma_start(out=rows[:], in_=source)
+            return rows
+
+        f_sb = load_rows("f_sb", f_prime)
+        n_sb = load_rows("n_sb", n_prev)
+        i_sb = load_rows("i_sb", i_prime)
+
+        acts = keep.tile([P, 2 * K], BF16)
+        nc.sync.dma_start(out=acts[:, 0:K], in_=x)
+        nc.sync.dma_start(out=acts[:, K : 2 * K], in_=h_prev)
+
+        weight_rows = {}
+        for gate, s in half_gates:
+            rows = keep.tile([P, 4 * K], BF16, name="rows_%s%d" % (gate, s))
+            for side_index, side in enumerate(sides):
+                nc.sync.dma_start(
+                    out=rows[:, side_index * 2 * K : (side_index + 1) * 2 * K],
+                    in_=weights[gate, side].rearrange("(s p j) k -> s p (j k)", s=2, j=2)[s],
+                )
+            weight_rows[gate, s] = rows
+        c_sb = load_rows("c_sb", c_prev)
+
+        bias_turned = turned_pool.tile([P, 2 * WORDS], F32, tag="bank")
+        nc.tensor.transpose(bias_turned[:, 0:P], bias_rows[:].bitcast(F32), ident[:])
+        bias_words = keep.tile([P, 4], F32)
+        nc.vector.tensor_copy(out=bias_words[:], in_=bias_turned[:, 0:4])
+        bias_spread = turned_pool.tile([P, 2 * WORDS], F32, tag="bank")
+        for r in range(4):
+            nc.tensor.transpose(
+                bias_spread[:, r * P : (r + 1) * P],
+                bias_words[:, r : r + 1].to_broadcast([P, P]),
+                ident[:],
+            )
+        bias_all = keep.tile([P, 2 * H], BF16)
+        nc.scalar.copy(out=bias_all[:].bitcast(F32), in_=bias_spread[:])
+        bias = {"z": bias_all[:, 0:H], "o": bias_all[:, H : 2 * H]}
+
+        n_t = keep.tile([P, H], F32)
+        nc.vector.tensor_tensor(out=n_t[:], in0=f_sb[:], in1=n_sb[:], op=ALU.mult)
+        nc.vector.tensor_tensor(out=n_t[:], in0=n_t[:], in1=i_sb[:], op=ALU.add)
+        nc.vector.tensor_scalar_max(out=n_t[:], in0=n_t[:], scalar1=1e-6)
+        n_inverse = keep.tile([P, H], F32)
+
+        def invert(quarter):
+            columns = slice(quarter * H // QUARTERS, (quarter + 1) * H // QUARTERS)
+            nc.vector.reciprocal(out=n_inverse[:, columns], in_=n_t[:, columns])
+
+        invert(0)
+
+        act_codes = keep.tile([P, 2 * P], U32, align_bytes=64)
+        act_scales = keep.tile([P, 2 * P], U8, align_bytes=64)
+        act_grouped = turn_two_panels(nc, turned_pool, stage, ident, acts[:].bitcast(F32), 0)
+        nc.vector.quantize_mx(
+            out=act_codes[:].bitcast(FP8X4), scales=act_scales[:], in_=act_grouped[:]
+        )
+
+        grouped = {}
+        codes = {}
+        scales = {}
+
+        def turn_weights(gate, s):
+            words = weight_rows[gate, s][:].bitcast(F32)
+            for side_index, side in enumerate(sides):
+                grouped[gate, s, side] = turn_two_panels(
+                    nc, turned_pool, stage, ident, words, 2 * side_index
+                )
+
+        def quantise_weights(gate, s):
+            codes[gate, s] = keep.tile(
+                [P, 2 * HALF_GATE], U32, name="codes_%s%d" % (gate, s), align_bytes=64
+            )
+            scales[gate, s] = keep.tile(
+                [P, 2 * HALF_GATE], U8, name="scales_%s%d" % (gate, s), align_bytes=64
+            )
+            for side_index, side in enumerate(sides):
+                columns = slice(side_index * HALF_GATE, (side_index + 1) * HALF_GATE)
+                nc.vector.quantize_mx(
+                    out=codes[gate, s][:, columns].bitcast(FP8X4),
+                    scales=scales[gate, s][:, columns],
+                    in_=grouped[gate, s, side][:],
+                )
+
+        squashed = {
+            "z": keep.tile([P, H], F32, name="tanh_z"),
+            "o": keep.tile([P, H], F32, name="tanh_o"),
+        }
+
+        def squash(gate, s):
+            acc = sums.tile([P, HALF_GATE], F32)
+            for side_index in range(len(sides)):
+                columns = slice(side_index * HALF_GATE, (side_index + 1) * HALF_GATE)
+                nc.tensor.matmul_mx(
+                    out=acc[:],
+                    lhsT=act_codes[:, side_index * P : (side_index + 1) * P].bitcast(FP8X4),
+                    lhsT_scale=act_scales[:, side_index * P : (side_index + 1) * P],
+                    rhs=codes[gate, s][:, columns].bitcast(FP8X4),
+                    rhs_scale=scales[gate, s][:, columns],
+                    start=(side_index == 0),
+                    stop=(side_index == len(sides) - 1),
+                )
+            outputs = slice(s * HALF_GATE, (s + 1) * HALF_GATE)
+            affine = stage.tile([P, HALF_GATE], F32)
+            nc.vector.tensor_tensor(
+                out=affine[:].rearrange("b (p j) -> b p j", j=2),
+                in0=acc[:].rearrange("b (j p) -> b p j", j=2),
+                in1=bias[gate][:, outputs].rearrange("b (p j) -> b p j", j=2),
+                op=ALU.add,
+            )
+            nc.scalar.activation(
+                out=squashed[gate][:, outputs], in_=affine[:], func=ACT.Tanh,
+                scale=(1.0 if gate == "z" else 0.5),
+            )
+
+        kept = keep.tile([P, H], F32)
+        nc.gpsimd.tensor_tensor(out=kept[:], in0=f_sb[:], in1=c_sb[:], op=ALU.mult)
+        c_t = keep.tile([P, H], F32)
+        scaled_cell = keep.tile([P, H], F32)
+        h_t = keep.tile([P, H], F32)
+
+        def cell(s):
+            outputs = slice(s * HALF_GATE, (s + 1) * HALF_GATE)
+            fresh = stage.tile([P, HALF_GATE], F32)
+            nc.gpsimd.tensor_tensor(
+                out=fresh[:], in0=i_sb[:, outputs], in1=squashed["z"][:, outputs], op=ALU.mult
+            )
+            nc.gpsimd.tensor_tensor(
+                out=c_t[:, outputs], in0=kept[:, outputs], in1=fresh[:], op=ALU.add
+            )
+            nc.sync.dma_start(out=out_1[:, outputs], in_=c_t[:, outputs])
+
+        def scale_cell(s):
+            outputs = slice(s * HALF_GATE, (s + 1) * HALF_GATE)
+            nc.vector.scalar_tensor_tensor(
+                out=scaled_cell[:, outputs], in0=c_t[:, outputs], scalar=0.5,
+                in1=n_inverse[:, outputs], op0=ALU.mult, op1=ALU.mult,
+            )
+
+        def readout(s):
+            outputs = slice(s * HALF_GATE, (s + 1) * HALF_GATE)
+            nc.vector.scalar_tensor_tensor(
+                out=h_t[:, outputs], in0=squashed["o"][:, outputs], scalar=1.0,
+                in1=scaled_cell[:, outputs], op0=ALU.add, op1=ALU.mult,
+            )
+            nc.sync.dma_start(out=out_0[:, outputs], in_=h_t[:, outputs])
+
+        count = len(half_gates)
+
+        def at(index):
+            return half_gates[index] if 0 <= index < count else None
+
+        for tick in range(count + 4):
+            if at(tick):
+                turn_weights(*at(tick))
+            if 1 <= tick < QUARTERS:
+                invert(tick)
+            if at(tick - 1):
+                quantise_weights(*at(tick - 1))
+            if at(tick - 2):
+                squash(*at(tick - 2))
+                if at(tick - 2)[0] == "z":
+                    cell(at(tick - 2)[1])
+            if at(tick - 4):
+                if at(tick - 4)[0] == "z":
+                    scale_cell(at(tick - 4)[1])
+                else:
+                    readout(at(tick - 4)[1])

@@ -15,53 +15,37 @@ P = 128
 K = 512
 H = 512
 WORDS = K // 2
-HALF_GATE = 2 * P
-QUARTERS = 4
-PSUM_BANKS = 8
-SUM_BANKS = 2
+HALF = 2 * P
 
 FLOPS = 2 * P * (2 * K) * (2 * H)
-
-
-def turn_two_panels(nc, turned_pool, grouped_pool, ident, words, first_panel):
-    bank = turned_pool.tile([P, 2 * WORDS], F32)
-    for piece in range(4):
-        first_word = (first_panel + piece // 2) * WORDS + piece % 2
-        nc.tensor.transpose(
-            bank[:, piece * P : (piece + 1) * P],
-            words[:, first_word : first_word + WORDS - 1 : 2],
-            ident[:],
-        )
-    grouped = grouped_pool.tile([P, 4 * HALF_GATE], BF16, align_bytes=64)
-    nc.scalar.copy(
-        out=grouped[:].bitcast(F32).rearrange("q (a c u) -> q a c u", a=2, u=2),
-        in_=bank[:].rearrange("q (a u c) -> q a c u", a=2, u=2),
-    )
-    return grouped
 
 
 def tile_slstmlayer_pb_s_kernel(
     tc, x, h_prev, c_prev, n_prev, i_prime, f_prime, Wz_x, b_z, Wz_h, Wo_x, b_o, Wo_h, out_0, out_1
 ):
     nc = tc.nc
-    half_gates = (("z", 0), ("z", 1), ("o", 0), ("o", 1))
     weights = {("z", "x"): Wz_x, ("z", "h"): Wz_h, ("o", "x"): Wo_x, ("o", "h"): Wo_h}
-    sides = ("x", "h")
 
     with ExitStack() as ctx:
         keep = ctx.enter_context(tc.tile_pool(name="keep", bufs=1))
-        stage = ctx.enter_context(tc.tile_pool(name="stage", bufs=6))
-        turned_pool = ctx.enter_context(tc.psum_pool(name="turned", bufs=PSUM_BANKS - SUM_BANKS))
-        sums = ctx.enter_context(tc.psum_pool(name="sums", bufs=SUM_BANKS))
+        stage = ctx.enter_context(tc.tile_pool(name="stage", bufs=4))
+        turned = ctx.enter_context(tc.psum_pool(name="turned", bufs=6))
+        sums = ctx.enter_context(tc.psum_pool(name="sums", bufs=2))
         ctx.enter_context(tc.manual_schedule())
 
-        bias_rows = keep.tile([P, 2 * P], BF16)
-        nc.gpsimd.memset(bias_rows[:].bitcast(F32), 0.0)
+        bias_cols = {}
+        for gate, source in (("z", b_z), ("o", b_o)):
+            cols = keep.tile([P, 4], BF16, name="bias_cols_" + gate)
+            nc.scalar.dma_start(out=cols[:], in_=source.rearrange("(p j) -> p j", j=4))
+            bias_cols[gate] = cols
+
+        one = keep.tile([P, 1], F32)
+        nc.vector.memset(one[:], 1.0)
+        warm = keep.tile([P, 2], F32)
+        nc.scalar.activation(out=warm[:, 0:1], in_=one[:], func=ACT.Ln)
+
         ident = keep.tile([P, P], F32)
         make_identity(nc, ident[:])
-
-        nc.sync.dma_start(out=bias_rows[0:2, :], in_=b_z.rearrange("(r c) -> r c", r=2))
-        nc.sync.dma_start(out=bias_rows[2:4, :], in_=b_o.rearrange("(r c) -> r c", r=2))
 
         def load_rows(name, source):
             rows = keep.tile([P, H], BF16, name=name)
@@ -70,164 +54,214 @@ def tile_slstmlayer_pb_s_kernel(
 
         f_sb = load_rows("f_sb", f_prime)
         n_sb = load_rows("n_sb", n_prev)
-        i_sb = load_rows("i_sb", i_prime)
-
         acts = keep.tile([P, 2 * K], BF16)
         nc.sync.dma_start(out=acts[:, 0:K], in_=x)
         nc.sync.dma_start(out=acts[:, K : 2 * K], in_=h_prev)
+        i_sb = load_rows("i_sb", i_prime)
 
-        weight_rows = {}
-        for gate, s in half_gates:
-            rows = keep.tile([P, 4 * K], BF16, name="rows_%s%d" % (gate, s))
-            for side_index, side in enumerate(sides):
-                nc.sync.dma_start(
-                    out=rows[:, side_index * 2 * K : (side_index + 1) * 2 * K],
-                    in_=weights[gate, side].rearrange("(s p j) k -> s p (j k)", s=2, j=2)[s],
-                )
-            weight_rows[gate, s] = rows
-        c_sb = load_rows("c_sb", c_prev)
+        rows = {}
 
-        bias_turned = turned_pool.tile([P, 2 * WORDS], F32, tag="bank")
-        nc.tensor.transpose(bias_turned[:, 0:P], bias_rows[:].bitcast(F32), ident[:])
-        bias_words = keep.tile([P, 4], F32)
-        nc.vector.tensor_copy(out=bias_words[:], in_=bias_turned[:, 0:4])
-        bias_spread = turned_pool.tile([P, 2 * WORDS], F32, tag="bank")
-        for r in range(4):
-            nc.tensor.transpose(
-                bias_spread[:, r * P : (r + 1) * P],
-                bias_words[:, r : r + 1].to_broadcast([P, P]),
-                ident[:],
+        def load_weights(gate, s, side):
+            tile = keep.tile([P, 2 * K], BF16, name="rows_%s%d%s" % (gate, s, side))
+            nc.sync.dma_start(
+                out=tile[:],
+                in_=weights[gate, side].rearrange("(s p j) k -> s p (j k)", s=2, j=2)[s],
             )
-        bias_all = keep.tile([P, 2 * H], BF16)
-        nc.scalar.copy(out=bias_all[:].bitcast(F32), in_=bias_spread[:])
-        bias = {"z": bias_all[:, 0:H], "o": bias_all[:, H : 2 * H]}
+            rows[gate, s, side] = tile
+
+        for s in range(2):
+            for side in ("x", "h"):
+                load_weights("z", s, side)
+        c_sb = load_rows("c_sb", c_prev)
+        for s in range(2):
+            for side in ("x", "h"):
+                load_weights("o", s, side)
 
         n_t = keep.tile([P, H], F32)
-        nc.vector.tensor_tensor(out=n_t[:], in0=f_sb[:], in1=n_sb[:], op=ALU.mult)
-        nc.vector.tensor_tensor(out=n_t[:], in0=n_t[:], in1=i_sb[:], op=ALU.add)
-        nc.vector.tensor_scalar_max(out=n_t[:], in0=n_t[:], scalar1=1e-6)
+        halves = [slice(s * HALF, (s + 1) * HALF) for s in range(2)]
+        for cols in halves:
+            nc.vector.tensor_tensor(out=n_t[:, cols], in0=f_sb[:, cols], in1=n_sb[:, cols], op=ALU.mult)
+        for cols in halves:
+            nc.vector.tensor_tensor(out=n_t[:, cols], in0=n_t[:, cols], in1=i_sb[:, cols], op=ALU.add)
+        for cols in halves:
+            nc.vector.tensor_scalar_max(out=n_t[:, cols], in0=n_t[:, cols], scalar1=1e-6)
+        n_log = keep.tile([P, H], F32)
         n_inverse = keep.tile([P, H], F32)
 
-        def invert(quarter):
-            columns = slice(quarter * H // QUARTERS, (quarter + 1) * H // QUARTERS)
-            nc.vector.reciprocal(out=n_inverse[:, columns], in_=n_t[:, columns])
+        bias_bank = turned.tile([P, 2 * WORDS], F32, name="bank")
+        for g, gate in enumerate(("z", "o")):
+            for r in range(2):
+                piece = 2 * g + r
+                nc.tensor.transpose(
+                    bias_bank[:, piece * P : (piece + 1) * P],
+                    bias_cols[gate][:].bitcast(F32)[:, r : r + 1].to_broadcast([P, P]),
+                    ident[:],
+                )
+        bias_all = keep.tile([P, 2 * H], BF16)
+        bias = {"z": bias_all[:, 0:H], "o": bias_all[:, H : 2 * H]}
 
-        invert(0)
+        def copy_bias():
+            nc.scalar.copy(
+                out=bias_all[:].bitcast(F32).rearrange("q (g n r) -> q g n r", g=2, r=2),
+                in_=bias_bank[:].rearrange("q (g r n) -> q g n r", g=2, r=2),
+            )
 
-        act_codes = keep.tile([P, 2 * P], U32, align_bytes=64)
-        act_scales = keep.tile([P, 2 * P], U8, align_bytes=64)
-        act_grouped = turn_two_panels(nc, turned_pool, stage, ident, acts[:].bitcast(F32), 0)
-        nc.vector.quantize_mx(
-            out=act_codes[:].bitcast(FP8X4), scales=act_scales[:], in_=act_grouped[:]
-        )
-
+        banks = {}
         grouped = {}
         codes = {}
         scales = {}
 
-        def turn_weights(gate, s):
-            words = weight_rows[gate, s][:].bitcast(F32)
-            for side_index, side in enumerate(sides):
-                grouped[gate, s, side] = turn_two_panels(
-                    nc, turned_pool, stage, ident, words, 2 * side_index
+        def turn(key):
+            words = (acts if key == "acts" else rows[key])[:].bitcast(F32)
+            bank = turned.tile([P, 2 * WORDS], F32, name="bank")
+            for piece in range(4):
+                first_word = (piece // 2) * WORDS + piece % 2
+                nc.tensor.transpose(
+                    bank[:, piece * P : (piece + 1) * P],
+                    words[:, first_word : first_word + WORDS - 1 : 2],
+                    ident[:],
                 )
+            banks[key] = bank
 
-        def quantise_weights(gate, s):
-            codes[gate, s] = keep.tile(
-                [P, 2 * HALF_GATE], U32, name="codes_%s%d" % (gate, s), align_bytes=64
+        def group(key, engine):
+            tile = stage.tile([P, 4 * HALF], BF16, name="grouped", align_bytes=64)
+            out = tile[:].bitcast(F32).rearrange("q (a c u) -> q a c u", a=2, u=2)
+            in_ = banks[key][:].rearrange("q (a u c) -> q a c u", a=2, u=2)
+            if engine == "scalar":
+                nc.scalar.copy(out=out, in_=in_)
+            else:
+                nc.vector.tensor_copy(out=out, in_=in_)
+            grouped[key] = tile
+
+        def quantise(key):
+            tag = "acts" if key == "acts" else "%s%d%s" % key
+            codes[key] = keep.tile([P, HALF], U32, name="codes_" + tag, align_bytes=64)
+            scales[key] = keep.tile([P, HALF], U8, name="scales_" + tag, align_bytes=64)
+            nc.vector.quantize_mx(
+                out=codes[key][:].bitcast(FP8X4), scales=scales[key][:], in_=grouped[key][:]
             )
-            scales[gate, s] = keep.tile(
-                [P, 2 * HALF_GATE], U8, name="scales_%s%d" % (gate, s), align_bytes=64
+
+        acc = {}
+
+        def multiply(gate, s, side):
+            if side == "x":
+                acc[gate, s] = sums.tile([P, HALF], F32, name="acc")
+            first = 0 if side == "x" else P
+            nc.tensor.matmul_mx(
+                out=acc[gate, s][:],
+                lhsT=codes["acts"][:, first : first + P].bitcast(FP8X4),
+                lhsT_scale=scales["acts"][:, first : first + P],
+                rhs=codes[gate, s, side][:].bitcast(FP8X4),
+                rhs_scale=scales[gate, s, side][:],
+                start=(side == "x"),
+                stop=(side == "h"),
             )
-            for side_index, side in enumerate(sides):
-                columns = slice(side_index * HALF_GATE, (side_index + 1) * HALF_GATE)
-                nc.vector.quantize_mx(
-                    out=codes[gate, s][:, columns].bitcast(FP8X4),
-                    scales=scales[gate, s][:, columns],
-                    in_=grouped[gate, s, side][:],
-                )
 
         squashed = {
             "z": keep.tile([P, H], F32, name="tanh_z"),
             "o": keep.tile([P, H], F32, name="tanh_o"),
         }
+        affine = {}
 
-        def squash(gate, s):
-            acc = sums.tile([P, HALF_GATE], F32)
-            for side_index in range(len(sides)):
-                columns = slice(side_index * HALF_GATE, (side_index + 1) * HALF_GATE)
-                nc.tensor.matmul_mx(
-                    out=acc[:],
-                    lhsT=act_codes[:, side_index * P : (side_index + 1) * P].bitcast(FP8X4),
-                    lhsT_scale=act_scales[:, side_index * P : (side_index + 1) * P],
-                    rhs=codes[gate, s][:, columns].bitcast(FP8X4),
-                    rhs_scale=scales[gate, s][:, columns],
-                    start=(side_index == 0),
-                    stop=(side_index == len(sides) - 1),
-                )
-            outputs = slice(s * HALF_GATE, (s + 1) * HALF_GATE)
-            affine = stage.tile([P, HALF_GATE], F32)
+        def add_bias(gate, s):
+            tile = stage.tile([P, HALF], F32, name="affine")
             nc.vector.tensor_tensor(
-                out=affine[:].rearrange("b (p j) -> b p j", j=2),
-                in0=acc[:].rearrange("b (j p) -> b p j", j=2),
-                in1=bias[gate][:, outputs].rearrange("b (p j) -> b p j", j=2),
+                out=tile[:].rearrange("b (p j) -> b p j", j=2),
+                in0=acc[gate, s][:].rearrange("b (j p) -> b p j", j=2),
+                in1=bias[gate][:, halves[s]].rearrange("b (p j) -> b p j", j=2),
                 op=ALU.add,
             )
+            affine[gate, s] = tile
+
+        def squash(gate, s):
             nc.scalar.activation(
-                out=squashed[gate][:, outputs], in_=affine[:], func=ACT.Tanh,
+                out=squashed[gate][:, halves[s]], in_=affine[gate, s][:], func=ACT.Tanh,
                 scale=(1.0 if gate == "z" else 0.5),
             )
 
         kept = keep.tile([P, H], F32)
-        nc.gpsimd.tensor_tensor(out=kept[:], in0=f_sb[:], in1=c_sb[:], op=ALU.mult)
         c_t = keep.tile([P, H], F32)
         scaled_cell = keep.tile([P, H], F32)
         h_t = keep.tile([P, H], F32)
 
         def cell(s):
-            outputs = slice(s * HALF_GATE, (s + 1) * HALF_GATE)
-            fresh = stage.tile([P, HALF_GATE], F32)
+            fresh = stage.tile([P, HALF], F32, name="fresh")
             nc.gpsimd.tensor_tensor(
-                out=fresh[:], in0=i_sb[:, outputs], in1=squashed["z"][:, outputs], op=ALU.mult
+                out=fresh[:], in0=i_sb[:, halves[s]], in1=squashed["z"][:, halves[s]], op=ALU.mult
             )
             nc.gpsimd.tensor_tensor(
-                out=c_t[:, outputs], in0=kept[:, outputs], in1=fresh[:], op=ALU.add
+                out=c_t[:, halves[s]], in0=kept[:, halves[s]], in1=fresh[:], op=ALU.add
             )
-            nc.sync.dma_start(out=out_1[:, outputs], in_=c_t[:, outputs])
+            nc.sync.dma_start(out=out_1[:, halves[s]], in_=c_t[:, halves[s]])
 
         def scale_cell(s):
-            outputs = slice(s * HALF_GATE, (s + 1) * HALF_GATE)
             nc.vector.scalar_tensor_tensor(
-                out=scaled_cell[:, outputs], in0=c_t[:, outputs], scalar=0.5,
-                in1=n_inverse[:, outputs], op0=ALU.mult, op1=ALU.mult,
+                out=scaled_cell[:, halves[s]], in0=c_t[:, halves[s]], scalar=0.5,
+                in1=n_inverse[:, halves[s]], op0=ALU.mult, op1=ALU.mult,
             )
 
         def readout(s):
-            outputs = slice(s * HALF_GATE, (s + 1) * HALF_GATE)
             nc.vector.scalar_tensor_tensor(
-                out=h_t[:, outputs], in0=squashed["o"][:, outputs], scalar=1.0,
-                in1=scaled_cell[:, outputs], op0=ALU.add, op1=ALU.mult,
+                out=h_t[:, halves[s]], in0=squashed["o"][:, halves[s]], scalar=1.0,
+                in1=scaled_cell[:, halves[s]], op0=ALU.add, op1=ALU.mult,
             )
-            nc.sync.dma_start(out=out_0[:, outputs], in_=h_t[:, outputs])
+            nc.sync.dma_start(out=out_0[:, halves[s]], in_=h_t[:, halves[s]])
 
-        count = len(half_gates)
+        z0x, z0h, z1x, z1h = [("z", s, side) for s in range(2) for side in ("x", "h")]
+        o0x, o0h, o1x, o1h = [("o", s, side) for s in range(2) for side in ("x", "h")]
 
-        def at(index):
-            return half_gates[index] if 0 <= index < count else None
-
-        for tick in range(count + 4):
-            if at(tick):
-                turn_weights(*at(tick))
-            if 1 <= tick < QUARTERS:
-                invert(tick)
-            if at(tick - 1):
-                quantise_weights(*at(tick - 1))
-            if at(tick - 2):
-                squash(*at(tick - 2))
-                if at(tick - 2)[0] == "z":
-                    cell(at(tick - 2)[1])
-            if at(tick - 4):
-                if at(tick - 4)[0] == "z":
-                    scale_cell(at(tick - 4)[1])
-                else:
-                    readout(at(tick - 4)[1])
+        copy_bias()
+        turn("acts")
+        group("acts", "scalar")
+        for cols in halves:
+            nc.scalar.activation(out=n_log[:, cols], in_=n_t[:, cols], func=ACT.Ln)
+        turn(z0x)
+        group(z0x, "vector")
+        quantise("acts")
+        turn(z0h)
+        group(z0h, "scalar")
+        quantise(z0x)
+        turn(z1x)
+        group(z1x, "vector")
+        turn(z1h)
+        group(z1h, "scalar")
+        quantise(z0h)
+        nc.scalar.activation(out=warm[:, 1:2], in_=one[:], func=ACT.Tanh)
+        quantise(z1x)
+        multiply(*z0x)
+        multiply(*z0h)
+        turn(o0x)
+        turn(o0h)
+        quantise(z1h)
+        group(o0x, "vector")
+        add_bias("z", 0)
+        squash("z", 0)
+        quantise(o0x)
+        multiply(*z1x)
+        multiply(*z1h)
+        turn(o1x)
+        turn(o1h)
+        group(o1x, "scalar")
+        group(o0h, "vector")
+        add_bias("z", 1)
+        squash("z", 1)
+        quantise(o0h)
+        group(o1h, "scalar")
+        nc.gpsimd.tensor_tensor(out=kept[:], in0=f_sb[:], in1=c_sb[:], op=ALU.mult)
+        cell(0)
+        cell(1)
+        nc.scalar.activation(out=n_inverse[:], in_=n_log[:], func=ACT.Exp, scale=-1.0)
+        quantise(o1x)
+        multiply(*o0x)
+        multiply(*o0h)
+        multiply(*o1x)
+        quantise(o1h)
+        multiply(*o1h)
+        add_bias("o", 0)
+        squash("o", 0)
+        scale_cell(0)
+        add_bias("o", 1)
+        squash("o", 1)
+        readout(0)
+        scale_cell(1)
+        readout(1)

@@ -184,13 +184,17 @@ def tile_slstmlayer_pb_s_kernel(
         scaled_cell = keep.tile([P, H], F32)
         h_t = keep.tile([P, H], F32)
 
-        def cell(s):
-            fresh = stage.tile([P, HALF], F32, name="fresh")
-            nc.gpsimd.tensor_tensor(
-                out=fresh[:], in0=i_sb[:, halves[s]], in1=squashed["z"][:, halves[s]], op=ALU.mult
+        fresh = keep.tile([P, H], F32)
+
+        def gate_cell(s):
+            nc.vector.tensor_tensor(
+                out=fresh[:, halves[s]], in0=i_sb[:, halves[s]], in1=squashed["z"][:, halves[s]],
+                op=ALU.mult,
             )
-            nc.gpsimd.tensor_tensor(
-                out=c_t[:, halves[s]], in0=kept[:, halves[s]], in1=fresh[:], op=ALU.add
+
+        def cell(s):
+            nc.vector.tensor_tensor(
+                out=c_t[:, halves[s]], in0=kept[:, halves[s]], in1=fresh[:, halves[s]], op=ALU.add
             )
             nc.sync.dma_start(out=out_1[:, halves[s]], in_=c_t[:, halves[s]])
 
@@ -222,46 +226,48 @@ def tile_slstmlayer_pb_s_kernel(
         group(z0h, "scalar")
         quantise(z0x)
         turn(z1x)
-        group(z1x, "vector")
-        turn(z1h)
-        group(z1h, "scalar")
-        quantise(z0h)
+        group(z1x, "scalar")
         nc.scalar.activation(out=warm[:, 1:2], in_=one[:], func=ACT.Tanh)
-        quantise(z1x)
+        turn(z1h)
+        quantise(z0h)
+        group(z1h, "vector")
         multiply(*z0x)
-        multiply(*z0h)
         turn(o0x)
+        multiply(*z0h)
+        quantise(z1x)
+        nc.vector.tensor_tensor(out=kept[:], in0=f_sb[:], in1=c_sb[:], op=ALU.mult)
         turn(o0h)
-        quantise(z1h)
-        group(o0x, "vector")
         add_bias("z", 0)
         squash("z", 0)
-        quantise(o0x)
+        quantise(z1h)
+        group(o0x, "vector")
         multiply(*z1x)
         multiply(*z1h)
         turn(o1x)
         turn(o1h)
+        group(o0h, "scalar")
         group(o1x, "scalar")
-        group(o0h, "vector")
+        gate_cell(0)
+        quantise(o0x)
         add_bias("z", 1)
-        squash("z", 1)
-        quantise(o0h)
-        group(o1h, "scalar")
-        nc.gpsimd.tensor_tensor(out=kept[:], in0=f_sb[:], in1=c_sb[:], op=ALU.mult)
         cell(0)
-        cell(1)
+        squash("z", 1)
+        group(o1h, "scalar")
         nc.scalar.activation(out=n_inverse[:], in_=n_log[:], func=ACT.Exp, scale=-1.0)
+        quantise(o0h)
         quantise(o1x)
         multiply(*o0x)
         multiply(*o0h)
-        multiply(*o1x)
+        gate_cell(1)
         quantise(o1h)
+        cell(1)
+        multiply(*o1x)
         multiply(*o1h)
+        scale_cell(0)
         add_bias("o", 0)
         squash("o", 0)
-        scale_cell(0)
+        scale_cell(1)
         add_bias("o", 1)
         squash("o", 1)
         readout(0)
-        scale_cell(1)
         readout(1)

@@ -29,18 +29,17 @@ def tile_slstmlayer_pb_s_kernel(
     with ExitStack() as ctx:
         keep = ctx.enter_context(tc.tile_pool(name="keep", bufs=1))
         stage = ctx.enter_context(tc.tile_pool(name="stage", bufs=4))
-        turned = ctx.enter_context(tc.psum_pool(name="turned", bufs=6))
-        sums = ctx.enter_context(tc.psum_pool(name="sums", bufs=2))
+        turned = ctx.enter_context(tc.psum_pool(name="turned", bufs=5))
+        sums = ctx.enter_context(tc.psum_pool(name="sums", bufs=3))
         ctx.enter_context(tc.manual_schedule())
 
-        bias_cols = {}
-        for gate, source in (("z", b_z), ("o", b_o)):
-            cols = keep.tile([P, 4], BF16, name="bias_cols_" + gate)
-            nc.scalar.dma_start(out=cols[:], in_=source.rearrange("(p j) -> p j", j=4))
-            bias_cols[gate] = cols
-
+        bias_rows = keep.tile([P, 2 * P], BF16)
+        nc.vector.memset(bias_rows[:].bitcast(F32), 0.0)
         one = keep.tile([P, 1], F32)
         nc.vector.memset(one[:], 1.0)
+        nc.scalar.dma_start(out=bias_rows[0:2, :], in_=b_z.rearrange("(s c) -> s c", s=2))
+        nc.scalar.dma_start(out=bias_rows[2:4, :], in_=b_o.rearrange("(s c) -> s c", s=2))
+
         warm = keep.tile([P, 2], F32)
         nc.scalar.activation(out=warm[:, 0:1], in_=one[:], func=ACT.Ln)
 
@@ -72,10 +71,22 @@ def tile_slstmlayer_pb_s_kernel(
         for s in range(2):
             for side in ("x", "h"):
                 load_weights("z", s, side)
+        for side in ("x", "h"):
+            load_weights("o", 0, side)
         c_sb = load_rows("c_sb", c_prev)
-        for s in range(2):
-            for side in ("x", "h"):
-                load_weights("o", s, side)
+        for side in ("x", "h"):
+            load_weights("o", 1, side)
+
+        bias = keep.tile([P, 8], F32)
+
+        def spread_bias():
+            bank = turned.tile([P, 2 * WORDS], F32, name="bank")
+            nc.tensor.transpose(bank[:, 0:P], bias_rows[:].bitcast(F32), ident[:])
+            words = keep.tile([P, 4], F32, name="bias_words")
+            nc.vector.tensor_copy(out=words[:], in_=bank[:, 0:4])
+            pairs = words[:].bitcast(BF16)
+            nc.vector.tensor_copy(out=bias[:, 0:4], in_=pairs[:, 0:4])
+            nc.vector.tensor_scalar_mul(out=bias[:, 4:8], in0=pairs[:, 4:8], scalar1=0.5)
 
         n_t = keep.tile([P, H], F32)
         halves = [slice(s * HALF, (s + 1) * HALF) for s in range(2)]
@@ -87,24 +98,6 @@ def tile_slstmlayer_pb_s_kernel(
             nc.vector.tensor_scalar_max(out=n_t[:, cols], in0=n_t[:, cols], scalar1=1e-6)
         n_log = keep.tile([P, H], F32)
         n_inverse = keep.tile([P, H], F32)
-
-        bias_bank = turned.tile([P, 2 * WORDS], F32, name="bank")
-        for g, gate in enumerate(("z", "o")):
-            for r in range(2):
-                piece = 2 * g + r
-                nc.tensor.transpose(
-                    bias_bank[:, piece * P : (piece + 1) * P],
-                    bias_cols[gate][:].bitcast(F32)[:, r : r + 1].to_broadcast([P, P]),
-                    ident[:],
-                )
-        bias_all = keep.tile([P, 2 * H], BF16)
-        bias = {"z": bias_all[:, 0:H], "o": bias_all[:, H : 2 * H]}
-
-        def copy_bias():
-            nc.scalar.copy(
-                out=bias_all[:].bitcast(F32).rearrange("q (g n r) -> q g n r", g=2, r=2),
-                in_=bias_bank[:].rearrange("q (g r n) -> q g n r", g=2, r=2),
-            )
 
         banks = {}
         grouped = {}
@@ -141,43 +134,50 @@ def tile_slstmlayer_pb_s_kernel(
                 out=codes[key][:].bitcast(FP8X4), scales=scales[key][:], in_=grouped[key][:]
             )
 
-        acc = {}
+        sums_bank = {}
+        squashed = {}
 
-        def multiply(gate, s, side):
-            if side == "x":
-                acc[gate, s] = sums.tile([P, HALF], F32, name="acc")
-            first = 0 if side == "x" else P
-            nc.tensor.matmul_mx(
-                out=acc[gate, s][:],
-                lhsT=codes["acts"][:, first : first + P].bitcast(FP8X4),
-                lhsT_scale=scales["acts"][:, first : first + P],
-                rhs=codes[gate, s, side][:].bitcast(FP8X4),
-                rhs_scale=scales[gate, s, side][:],
-                start=(side == "x"),
-                stop=(side == "h"),
-            )
-
-        squashed = {
-            "z": keep.tile([P, H], F32, name="tanh_z"),
-            "o": keep.tile([P, H], F32, name="tanh_o"),
-        }
-        affine = {}
-
-        def add_bias(gate, s):
-            tile = stage.tile([P, HALF], F32, name="affine")
-            nc.vector.tensor_tensor(
-                out=tile[:].rearrange("b (p j) -> b p j", j=2),
-                in0=acc[gate, s][:].rearrange("b (j p) -> b p j", j=2),
-                in1=bias[gate][:, halves[s]].rearrange("b (p j) -> b p j", j=2),
-                op=ALU.add,
-            )
-            affine[gate, s] = tile
+        def multiply(gate, s):
+            bank = sums.tile([P, 2 * HALF], F32, name="sums_bank")
+            for j in range(2):
+                panel = slice(j * P, (j + 1) * P)
+                for side in ("x", "h"):
+                    first = 0 if side == "x" else P
+                    nc.tensor.matmul_mx(
+                        out=bank[:, panel],
+                        lhsT=codes[gate, s, side][:, panel].bitcast(FP8X4),
+                        lhsT_scale=scales[gate, s, side][:, panel],
+                        rhs=codes["acts"][:, first : first + P].bitcast(FP8X4),
+                        rhs_scale=scales["acts"][:, first : first + P],
+                        start=(side == "x"),
+                        stop=(side == "h"),
+                    )
+            sums_bank[gate, s] = bank
 
         def squash(gate, s):
-            nc.scalar.activation(
-                out=squashed[gate][:, halves[s]], in_=affine[gate, s][:], func=ACT.Tanh,
-                scale=(1.0 if gate == "z" else 0.5),
-            )
+            tile = keep.tile([P, HALF], F32, name="squashed_%s%d" % (gate, s))
+            for j in range(2):
+                panel = slice(j * P, (j + 1) * P)
+                column = 4 * (gate == "o") + 2 * s + j
+                nc.scalar.activation(
+                    out=tile[:, panel], in_=sums_bank[gate, s][:, panel], func=ACT.Tanh,
+                    bias=bias[:, column : column + 1], scale=(1.0 if gate == "z" else 0.5),
+                )
+            squashed[gate, s] = tile
+
+        def turn_back(gate, s):
+            for j in range(2):
+                nc.tensor.transpose(
+                    sums_bank[gate, s][:, HALF + j * P : HALF + (j + 1) * P],
+                    squashed[gate, s][:, j * P : (j + 1) * P],
+                    ident[:],
+                )
+
+        def in_order(gate, s):
+            return sums_bank[gate, s][:, HALF : 2 * HALF].rearrange("b (j p) -> b p j", j=2)
+
+        def pairs_of(ap):
+            return ap.rearrange("b (p j) -> b p j", j=2)
 
         kept = keep.tile([P, H], F32)
         c_t = keep.tile([P, H], F32)
@@ -188,8 +188,8 @@ def tile_slstmlayer_pb_s_kernel(
 
         def gate_cell(s):
             nc.vector.tensor_tensor(
-                out=fresh[:, halves[s]], in0=i_sb[:, halves[s]], in1=squashed["z"][:, halves[s]],
-                op=ALU.mult,
+                out=pairs_of(fresh[:, halves[s]]), in0=in_order("z", s),
+                in1=pairs_of(i_sb[:, halves[s]]), op=ALU.mult,
             )
 
         def cell(s):
@@ -206,68 +206,70 @@ def tile_slstmlayer_pb_s_kernel(
 
         def readout(s):
             nc.vector.scalar_tensor_tensor(
-                out=h_t[:, halves[s]], in0=squashed["o"][:, halves[s]], scalar=1.0,
-                in1=scaled_cell[:, halves[s]], op0=ALU.add, op1=ALU.mult,
+                out=pairs_of(h_t[:, halves[s]]), in0=in_order("o", s), scalar=1.0,
+                in1=pairs_of(scaled_cell[:, halves[s]]), op0=ALU.add, op1=ALU.mult,
             )
             nc.sync.dma_start(out=out_0[:, halves[s]], in_=h_t[:, halves[s]])
 
         z0x, z0h, z1x, z1h = [("z", s, side) for s in range(2) for side in ("x", "h")]
         o0x, o0h, o1x, o1h = [("o", s, side) for s in range(2) for side in ("x", "h")]
 
-        copy_bias()
+        def invert(s):
+            nc.scalar.activation(
+                out=n_inverse[:, halves[s]], in_=n_log[:, halves[s]], func=ACT.Exp, scale=-1.0
+            )
+
         turn("acts")
+        spread_bias()
         group("acts", "scalar")
         for cols in halves:
             nc.scalar.activation(out=n_log[:, cols], in_=n_t[:, cols], func=ACT.Ln)
         turn(z0x)
-        group(z0x, "vector")
         quantise("acts")
+        group(z0x, "vector")
         turn(z0h)
         group(z0h, "scalar")
-        quantise(z0x)
-        turn(z1x)
-        group(z1x, "scalar")
         nc.scalar.activation(out=warm[:, 1:2], in_=one[:], func=ACT.Tanh)
-        turn(z1h)
+        turn(z1x)
+        quantise(z0x)
         quantise(z0h)
-        group(z1h, "vector")
-        multiply(*z0x)
+        group(z1x, "vector")
+        turn(z1h)
+        multiply("z", 0)
+        squash("z", 0)
         turn(o0x)
-        multiply(*z0h)
         quantise(z1x)
         nc.vector.tensor_tensor(out=kept[:], in0=f_sb[:], in1=c_sb[:], op=ALU.mult)
-        turn(o0h)
-        add_bias("z", 0)
-        squash("z", 0)
-        quantise(z1h)
         group(o0x, "vector")
-        multiply(*z1x)
-        multiply(*z1h)
-        turn(o1x)
-        turn(o1h)
-        group(o0h, "scalar")
-        group(o1x, "scalar")
-        gate_cell(0)
+        turn(o0h)
+        group(z1h, "scalar")
         quantise(o0x)
-        add_bias("z", 1)
-        cell(0)
-        squash("z", 1)
-        group(o1h, "scalar")
-        nc.scalar.activation(out=n_inverse[:], in_=n_log[:], func=ACT.Exp, scale=-1.0)
+        group(o0h, "scalar")
+        turn(o1x)
+        turn_back("z", 0)
+        quantise(z1h)
+        group(o1x, "scalar")
+        turn(o1h)
+        multiply("z", 1)
         quantise(o0h)
+        gate_cell(0)
+        group(o1h, "scalar")
+        multiply("o", 0)
         quantise(o1x)
-        multiply(*o0x)
-        multiply(*o0h)
-        gate_cell(1)
+        squash("z", 1)
         quantise(o1h)
-        cell(1)
-        multiply(*o1x)
-        multiply(*o1h)
+        turn_back("z", 1)
+        cell(0)
+        invert(0)
         scale_cell(0)
-        add_bias("o", 0)
         squash("o", 0)
-        scale_cell(1)
-        add_bias("o", 1)
+        multiply("o", 1)
+        gate_cell(1)
+        invert(1)
+        cell(1)
+        turn_back("o", 0)
         squash("o", 1)
+        scale_cell(1)
         readout(0)
+        turn_back("o", 1)
         readout(1)

@@ -225,15 +225,15 @@ def tile_slstmlayer_pb_s_kernel(
         for cols in halves:
             nc.scalar.activation(out=n_log[:, cols], in_=n_t[:, cols], func=ACT.Ln)
         turn(z0x)
-        quantise("acts")
         group(z0x, "vector")
+        quantise("acts")
         turn(z0h)
         group(z0h, "scalar")
         nc.scalar.activation(out=warm[:, 1:2], in_=one[:], func=ACT.Tanh)
         turn(z1x)
         quantise(z0x)
-        quantise(z0h)
         group(z1x, "vector")
+        quantise(z0h)
         turn(z1h)
         multiply("z", 0)
         squash("z", 0)
@@ -243,11 +243,11 @@ def tile_slstmlayer_pb_s_kernel(
         group(o0x, "vector")
         turn(o0h)
         group(z1h, "scalar")
-        quantise(o0x)
+        quantise(z1h)
         group(o0h, "scalar")
         turn(o1x)
         turn_back("z", 0)
-        quantise(z1h)
+        quantise(o0x)
         group(o1x, "scalar")
         turn(o1h)
         multiply("z", 1)
@@ -261,15 +261,15 @@ def tile_slstmlayer_pb_s_kernel(
         turn_back("z", 1)
         cell(0)
         invert(0)
-        scale_cell(0)
         squash("o", 0)
         multiply("o", 1)
         gate_cell(1)
+        scale_cell(0)
         invert(1)
         cell(1)
         turn_back("o", 0)
         squash("o", 1)
-        scale_cell(1)
         readout(0)
+        scale_cell(1)
         turn_back("o", 1)
         readout(1)

from contextlib import ExitStack

import concourse.mybir as mybir
from concourse.masks import make_identity

F32 = mybir.dt.float32
BF16 = mybir.dt.bfloat16
U32 = mybir.dt.uint32
U8 = mybir.dt.uint8
FP8X4 = mybir.dt.float8_e4m3fn_x4
ALU = mybir.AluOpType
ACT = mybir.ActivationFunctionType

P = 128
K = 512
H = 512
WORDS = K // 2
HALF = 2 * P

FLOPS = 2 * P * (2 * K) * (2 * H)


def tile_slstmlayer_pb_s_kernel(
    tc, x, h_prev, c_prev, n_prev, i_prime, f_prime, Wz_x, b_z, Wz_h, Wo_x, b_o, Wo_h, out_0, out_1
):
    nc = tc.nc
    weights = {("z", "x"): Wz_x, ("z", "h"): Wz_h, ("o", "x"): Wo_x, ("o", "h"): Wo_h}

    with ExitStack() as ctx:
        keep = ctx.enter_context(tc.tile_pool(name="keep", bufs=1))
        stage = ctx.enter_context(tc.tile_pool(name="stage", bufs=4))
        turned = ctx.enter_context(tc.psum_pool(name="turned", bufs=5))
        sums = ctx.enter_context(tc.psum_pool(name="sums", bufs=3))
        ctx.enter_context(tc.manual_schedule())

        bias_rows = keep.tile([P, 2 * P], BF16)
        nc.vector.memset(bias_rows[:].bitcast(F32), 0.0)
        one = keep.tile([P, 1], F32)
        nc.vector.memset(one[:], 1.0)
        nc.scalar.dma_start(out=bias_rows[0:2, :], in_=b_z.rearrange("(s c) -> s c", s=2))
        nc.scalar.dma_start(out=bias_rows[2:4, :], in_=b_o.rearrange("(s c) -> s c", s=2))

        warm = keep.tile([P, 2], F32)
        nc.scalar.activation(out=warm[:, 0:1], in_=one[:], func=ACT.Ln)

        ident = keep.tile([P, P], F32)
        make_identity(nc, ident[:])

        def load_rows(name, source):
            rows = keep.tile([P, H], BF16, name=name)
            nc.sync.dma_start(out=rows[:], in_=source)
            return rows

        f_sb = load_rows("f_sb", f_prime)
        n_sb = load_rows("n_sb", n_prev)
        acts = keep.tile([P, 2 * K], BF16)
        nc.sync.dma_start(out=acts[:, 0:K], in_=x)
        nc.sync.dma_start(out=acts[:, K : 2 * K], in_=h_prev)
        i_sb = load_rows("i_sb", i_prime)

        rows = {}

        def load_weights(gate, s, side):
            tile = keep.tile([P, 2 * K], BF16, name="rows_%s%d%s" % (gate, s, side))
            nc.sync.dma_start(
                out=tile[:],
                in_=weights[gate, side].rearrange("(s p j) k -> s p (j k)", s=2, j=2)[s],
            )
            rows[gate, s, side] = tile

        for s in range(2):
            for side in ("x", "h"):
                load_weights("z", s, side)
        for side in ("x", "h"):
            load_weights("o", 0, side)
        c_sb = load_rows("c_sb", c_prev)
        for side in ("x", "h"):
            load_weights("o", 1, side)

        bias = keep.tile([P, 8], F32)

        def spread_bias():
            bank = turned.tile([P, 2 * WORDS], F32, name="bank")
            nc.tensor.transpose(bank[:, 0:P], bias_rows[:].bitcast(F32), ident[:])
            words = keep.tile([P, 4], F32, name="bias_words")
            nc.vector.tensor_copy(out=words[:], in_=bank[:, 0:4])
            pairs = words[:].bitcast(BF16)
            nc.vector.tensor_copy(out=bias[:, 0:4], in_=pairs[:, 0:4])
            nc.vector.tensor_scalar_mul(out=bias[:, 4:8], in0=pairs[:, 4:8], scalar1=0.5)

        n_t = keep.tile([P, H], F32)
        halves = [slice(s * HALF, (s + 1) * HALF) for s in range(2)]
        for cols in halves:
            nc.vector.tensor_tensor(out=n_t[:, cols], in0=f_sb[:, cols], in1=n_sb[:, cols], op=ALU.mult)
        for cols in halves:
            nc.vector.tensor_tensor(out=n_t[:, cols], in0=n_t[:, cols], in1=i_sb[:, cols], op=ALU.add)
        for cols in halves:
            nc.vector.tensor_scalar_max(out=n_t[:, cols], in0=n_t[:, cols], scalar1=1e-6)
        n_log = keep.tile([P, H], F32)
        n_inverse = keep.tile([P, H], F32)

        banks = {}
        grouped = {}
        codes = {}
        scales = {}

        def turn(key):
            words = (acts if key == "acts" else rows[key])[:].bitcast(F32)
            bank = turned.tile([P, 2 * WORDS], F32, name="bank")
            for piece in range(4):
                first_word = (piece // 2) * WORDS + piece % 2
                nc.tensor.transpose(
                    bank[:, piece * P : (piece + 1) * P],
                    words[:, first_word : first_word + WORDS - 1 : 2],
                    ident[:],
                )
            banks[key] = bank

        def group(key, engine):
            tile = stage.tile([P, 4 * HALF], BF16, name="grouped", align_bytes=64)
            out = tile[:].bitcast(F32).rearrange("q (a c u) -> q a c u", a=2, u=2)
            in_ = banks[key][:].rearrange("q (a u c) -> q a c u", a=2, u=2)
            if engine == "scalar":
                nc.scalar.copy(out=out, in_=in_)
            else:
                nc.vector.tensor_copy(out=out, in_=in_)
            grouped[key] = tile

        def quantise(key):
            tag = "acts" if key == "acts" else "%s%d%s" % key
            codes[key] = keep.tile([P, HALF], U32, name="codes_" + tag, align_bytes=64)
            scales[key] = keep.tile([P, HALF], U8, name="scales_" + tag, align_bytes=64)
            nc.vector.quantize_mx(
                out=codes[key][:].bitcast(FP8X4), scales=scales[key][:], in_=grouped[key][:]
            )

        sums_bank = {}
        squashed = {}

        def multiply(gate, s):
            bank = sums.tile([P, 2 * HALF], F32, name="sums_bank")
            for j in range(2):
                panel = slice(j * P, (j + 1) * P)
                for side in ("x", "h"):
                    first = 0 if side == "x" else P
                    nc.tensor.matmul_mx(
                        out=bank[:, panel],
                        lhsT=codes[gate, s, side][:, panel].bitcast(FP8X4),
                        lhsT_scale=scales[gate, s, side][:, panel],
                        rhs=codes["acts"][:, first : first + P].bitcast(FP8X4),
                        rhs_scale=scales["acts"][:, first : first + P],
                        start=(side == "x"),
                        stop=(side == "h"),
                    )
            sums_bank[gate, s] = bank

        def squash(gate, s):
            tile = keep.tile([P, HALF], F32, name="squashed_%s%d" % (gate, s))
            for j in range(2):
                panel = slice(j * P, (j + 1) * P)
                column = 4 * (gate == "o") + 2 * s + j
                nc.scalar.activation(
                    out=tile[:, panel], in_=sums_bank[gate, s][:, panel], func=ACT.Tanh,
                    bias=bias[:, column : column + 1], scale=(1.0 if gate == "z" else 0.5),
                )
            squashed[gate, s] = tile

        def turn_back(gate, s):
            for j in range(2):
                nc.tensor.transpose(
                    sums_bank[gate, s][:, HALF + j * P : HALF + (j + 1) * P],
                    squashed[gate, s][:, j * P : (j + 1) * P],
                    ident[:],
                )

        def in_order(gate, s):
            return sums_bank[gate, s][:, HALF : 2 * HALF].rearrange("b (j p) -> b p j", j=2)

        def pairs_of(ap):
            return ap.rearrange("b (p j) -> b p j", j=2)

        kept = keep.tile([P, H], F32)
        c_t = keep.tile([P, H], F32)
        scaled_cell = keep.tile([P, H], F32)
        h_t = keep.tile([P, H], F32)

        fresh = keep.tile([P, H], F32)

        def gate_cell(s):
            nc.vector.tensor_tensor(
                out=pairs_of(fresh[:, halves[s]]), in0=in_order("z", s),
                in1=pairs_of(i_sb[:, halves[s]]), op=ALU.mult,
            )

        def cell(s):
            nc.vector.tensor_tensor(
                out=c_t[:, halves[s]], in0=kept[:, halves[s]], in1=fresh[:, halves[s]], op=ALU.add
            )
            nc.sync.dma_start(out=out_1[:, halves[s]], in_=c_t[:, halves[s]])

        def scale_cell(s):
            nc.vector.scalar_tensor_tensor(
                out=scaled_cell[:, halves[s]], in0=c_t[:, halves[s]], scalar=0.5,
                in1=n_inverse[:, halves[s]], op0=ALU.mult, op1=ALU.mult,
            )

        def readout(s):
            nc.vector.scalar_tensor_tensor(
                out=pairs_of(h_t[:, halves[s]]), in0=in_order("o", s), scalar=1.0,
                in1=pairs_of(scaled_cell[:, halves[s]]), op0=ALU.add, op1=ALU.mult,
            )
            nc.sync.dma_start(out=out_0[:, halves[s]], in_=h_t[:, halves[s]])

        z0x, z0h, z1x, z1h = [("z", s, side) for s in range(2) for side in ("x", "h")]
        o0x, o0h, o1x, o1h = [("o", s, side) for s in range(2) for side in ("x", "h")]

        def invert(s):
            nc.scalar.activation(
                out=n_inverse[:, halves[s]], in_=n_log[:, halves[s]], func=ACT.Exp, scale=-1.0
            )

        turn("acts")
        spread_bias()
        group("acts", "scalar")
        for cols in halves:
            nc.scalar.activation(out=n_log[:, cols], in_=n_t[:, cols], func=ACT.Ln)
        turn(z0x)
        group(z0x, "vector")
        quantise("acts")
        turn(z0h)
        group(z0h, "scalar")
        nc.scalar.activation(out=warm[:, 1:2], in_=one[:], func=ACT.Tanh)
        turn(z1x)
        quantise(z0x)
        group(z1x, "vector")
        quantise(z0h)
        turn(z1h)
        multiply("z", 0)
        squash("z", 0)
        turn(o0x)
        quantise(z1x)
        nc.vector.tensor_tensor(out=kept[:], in0=f_sb[:], in1=c_sb[:], op=ALU.mult)
        group(o0x, "vector")
        turn(o0h)
        group(z1h, "scalar")
        quantise(z1h)
        group(o0h, "scalar")
        turn(o1x)
        turn_back("z", 0)
        quantise(o0x)
        group(o1x, "scalar")
        turn(o1h)
        multiply("z", 1)
        quantise(o0h)
        gate_cell(0)
        group(o1h, "scalar")
        multiply("o", 0)
        quantise(o1x)
        squash("z", 1)
        quantise(o1h)
        turn_back("z", 1)
        cell(0)
        invert(0)
        squash("o", 0)
        multiply("o", 1)
        gate_cell(1)
        scale_cell(0)
        invert(1)
        cell(1)
        turn_back("o", 0)
        squash("o", 1)
        readout(0)
        scale_cell(1)
        turn_back("o", 1)
        readout(1)
